import numpy as np
import ml_dtypes


def mxq(x, axis, fmt="e4m3"):
    dtype, down = {"e4m3": (ml_dtypes.float8_e4m3fn, 7), "e5m2": (ml_dtypes.float8_e5m2, 14)}[fmt]
    v = np.moveaxis(np.asarray(x, np.float32).astype(ml_dtypes.bfloat16).astype(np.float64), axis, -1)
    blocks = v.reshape(v.shape[:-1] + (-1, 32))
    amax = np.abs(blocks).max(-1, keepdims=True)
    byte = np.maximum(np.where(amax > 0, np.frexp(amax)[1] - 1 + 127, 0) - down, 1)
    scale = np.exp2(byte - 127.0)
    codes = (blocks / scale).astype(np.float32).astype(dtype).astype(np.float64)
    return np.moveaxis((codes * scale).reshape(v.shape), -1, axis)


WIDE = False


def mx_kscale(k):
    if not WIDE:
        return np.ones(k)
    levels = np.array([10, -10, 5, -5, 0])
    a = np.random.permutation(np.resize(levels, k // 512 * 4)).reshape(k // 512, 4)
    idx = np.arange(k)
    return np.exp2(a[idx // 512, idx % 128 // 32])


BF16 = ml_dtypes.bfloat16


def bf(x):
    return np.asarray(x, np.float32).astype(BF16)


def f64(x):
    return np.asarray(x).astype(np.float64)


E2M1 = np.array([0.0, 0.5, 1.0, 1.5, 2.0, 3.0, 4.0, 6.0, -0.0, -0.5, -1.0, -1.5, -2.0, -3.0, -4.0, -6.0])


def pack_weight(w, fmt):
    k, n = w.shape
    w = f64(bf(w)).reshape(k // 32, 32, n)
    amax = np.abs(w).max(1)
    if fmt == "e4m3":
        byte = np.frexp(amax)[1] - 1 + 127 - 7
    else:
        mant, ex = np.frexp(amax / 6.0)
        byte = np.where(mant > 0.5, ex, ex - 1) + 127
    byte = np.clip(np.where(amax > 0, byte, 1), 1, 254)
    scaled = (w * np.exp2(127.0 - byte)[:, None, :]).reshape(k, n).astype(np.float32)
    by_word = np.ascontiguousarray(scaled.reshape(k // 512, 128, 4, n).transpose(0, 1, 3, 2))
    if fmt == "e4m3":
        words = by_word.astype(ml_dtypes.float8_e4m3fn).view(np.uint8)
    else:
        c = by_word.astype(ml_dtypes.float4_e2m1fn).view(np.uint8) & 0xF
        words = c[..., 0::2] | (c[..., 1::2] << 4)
    return np.ascontiguousarray(words), np.ascontiguousarray(byte.astype(np.uint8).reshape(k // 512, 16, n))


def unpack_weight(words, scales, fmt):
    g, p, n, _ = words.shape
    if fmt == "e4m3":
        vals = np.ascontiguousarray(words).view(ml_dtypes.float8_e4m3fn).astype(np.float64)
    else:
        nib = np.empty((g, p, n, 4), np.uint8)
        nib[..., 0::2] = words & 0xF
        nib[..., 1::2] = words >> 4
        vals = E2M1[nib]
    vals = vals * np.repeat(np.exp2(scales.astype(np.float64) - 127.0), 8, axis=1)[..., None]
    return vals.transpose(0, 1, 3, 2).reshape(g * 512, n)


B, H, W, C, I, O, NH = 2, 16, 128, 1024, 512, 512, 8
DH = I // NH
SCALE = DH ** -0.5
FMT = "e4m3"


def setup_inputs():
    s, t = mx_kscale(C), mx_kscale(I)
    sc = s[None, :, None, None]
    left_feat = bf(np.random.standard_normal((B, C, H, W)) * sc)
    right_feat = bf(np.random.standard_normal((B, C, H, W)) * sc)
    wq = np.random.standard_normal((I, C)) / np.sqrt(C) / s[None, :] * t[:, None]
    wk = np.random.standard_normal((I, C)) / np.sqrt(C) / s[None, :] / t[:, None]
    wq_words, wq_scales = pack_weight(np.ascontiguousarray(wq.T), FMT)
    wk_words, wk_scales = pack_weight(np.ascontiguousarray(wk.T), FMT)
    return {"left_feat": left_feat,
            "right_feat": right_feat,
            "wq_words": wq_words, "wq_scales": wq_scales,
            "wk_words": wk_words, "wk_scales": wk_scales}


def reference(left_feat, right_feat, wq_words, wq_scales, wk_words, wk_scales):
    lf = f64(left_feat).reshape(B, C, H * W)
    rf = f64(right_feat).reshape(B, C, H * W)
    q = unpack_weight(wq_words, wq_scales, FMT).T @ mxq(lf, 1, "e4m3")
    k = unpack_weight(wk_words, wk_scales, FMT).T @ mxq(rf, 1, "e4m3")
    q = q.reshape(B, I, H, W).transpose(0, 2, 3, 1)
    k = k.reshape(B, I, H, W).transpose(0, 2, 1, 3)
    return (mxq(q, 3, "e4m3") @ mxq(k, 2, "e4m3")) * SCALE

@@ -1,0 +1,183 @@
+from contextlib import ExitStack
+
+import concourse.mybir as mybir
+
+BF16 = mybir.dt.bfloat16
+F32 = mybir.dt.float32
+I32 = mybir.dt.int32
+U32 = mybir.dt.uint32
+U8 = mybir.dt.uint8
+FP8X4 = mybir.dt.float8_e4m3fn_x4
+
+P = 128
+PACK = 4
+K_PASS = P * PACK
+
+BATCH, CHANNELS, IMAGE_ROWS, WIDTH = 2, 1024, 16, 128
+INNER = 512
+SCALE = 0.125
+
+C_PASSES = CHANNELS // K_PASS
+O_TILES = INNER // P
+assert O_TILES == PACK and INNER == K_PASS
+
+PIECE_ROWS = 4
+PIECE_COLS = PIECE_ROWS * WIDTH
+PIECES_PER_MAP = IMAGE_ROWS // PIECE_ROWS
+LEFT, RIGHT = 0, 1
+
+VECTOR_COLS = 384
+RUN = 4
+PREFETCH = 6
+
+FLOPS = 2 * (2 * BATCH * IMAGE_ROWS * WIDTH * CHANNELS * INNER) + 2 * BATCH * IMAGE_ROWS * WIDTH * WIDTH * INNER
+
+
+def tile_sttm_single_pa_t_kernel(
+    tc, left_feat, right_feat, wq_words, wq_scales, wk_words, wk_scales, out
+):
+    nc = tc.nc
+    maps = (left_feat, right_feat)
+    weight_inputs = ((wq_words, wq_scales), (wk_words, wk_scales))
+    pieces = [
+        (b, part, side) for b in range(BATCH) for part in range(PIECES_PER_MAP) for side in (LEFT, RIGHT)
+    ]
+
+    with ExitStack() as ctx:
+        weights = ctx.enter_context(tc.tile_pool(name="weights", bufs=1))
+        raw_pool = ctx.enter_context(tc.tile_pool(name="raw", bufs=C_PASSES * (PREFETCH + 2)))
+        grouped_pool = ctx.enter_context(tc.tile_pool(name="grouped", bufs=3))
+        map_mx_pool = ctx.enter_context(tc.tile_pool(name="map_mx", bufs=3))
+        proj_pool = ctx.enter_context(tc.tile_pool(name="proj", bufs=3))
+        proj_mx_pool = ctx.enter_context(tc.tile_pool(name="proj_mx", bufs=4))
+        dots_pool = ctx.enter_context(tc.tile_pool(name="dots", bufs=3))
+        proj_psum = ctx.enter_context(tc.psum_pool(name="proj_psum", bufs=6))
+        dots_psum = ctx.enter_context(tc.psum_pool(name="dots_psum", bufs=2))
+
+        w_codes = weights.tile([P, 2, C_PASSES, INNER], U32, align_bytes=64)
+        w_scales = weights.tile([P, 2, C_PASSES, INNER], U8, align_bytes=64)
+        nc.vector.memset(w_scales[:].rearrange("p s g n -> p (s g n)").bitcast(I32), 0)
+
+        raw = {}
+        grouped = {}
+        map_mx = {}
+        proj = {}
+        proj_mx = {}
+
+        def load_weight(side):
+            code_bytes, scale_bytes = weight_inputs[side]
+            for quadrant in range(4):
+                nc.sync.dma_start(
+                    out=w_scales[32 * quadrant : 32 * quadrant + 4, side, :, :].bitcast(I32),
+                    in_=scale_bytes[:, 4 * quadrant : 4 * quadrant + 4, :].rearrange("g r n -> r g n").bitcast(I32),
+                )
+            nc.sync.dma_start(
+                out=w_codes[:, side, :, :].bitcast(I32),
+                in_=code_bytes.rearrange("g p n t -> p g (n t)").bitcast(I32),
+            )
+
+        def load_map(n):
+            b, part, side = pieces[n]
+            by_pass = maps[side][b].rearrange("(g p j) h w -> g p j (h w)", p=P, j=PACK)
+            for g in range(C_PASSES):
+                rows = raw_pool.tile([P, PACK, PIECE_COLS], BF16)
+                nc.sync.dma_start(
+                    out=rows[:], in_=by_pass[g][:, :, part * PIECE_COLS : (part + 1) * PIECE_COLS]
+                )
+                raw[n, g] = rows
+
+        def regroup(n):
+            side_by_side = grouped_pool.tile([P, C_PASSES, PIECE_COLS, PACK], BF16, align_bytes=64)
+            grouped[n] = side_by_side
+            shares = (
+                (nc.vector.tensor_copy, slice(0, VECTOR_COLS)),
+                (nc.scalar.copy, slice(VECTOR_COLS, PIECE_COLS)),
+            )
+            for g in range(C_PASSES):
+                for copy, cols in shares:
+                    copy(
+                        out=side_by_side[:, g, cols, :].rearrange("p (c i) j -> p c j i", i=RUN),
+                        in_=raw[n, g][:, :, cols].rearrange("p j (c i) -> p c j i", i=RUN),
+                    )
+
+        def quantise_map(n):
+            codes = map_mx_pool.tile([P, C_PASSES, PIECE_COLS], U32, align_bytes=64, name="map_codes")
+            scales = map_mx_pool.tile([P, C_PASSES, PIECE_COLS], U8, align_bytes=64, name="map_scales")
+            nc.vector.quantize_mx(
+                out=codes[:].rearrange("p g c -> p (g c)").bitcast(FP8X4),
+                scales=scales[:].rearrange("p g c -> p (g c)"),
+                in_=grouped[n][:].rearrange("p g c j -> p (g c j)"),
+            )
+            map_mx[n] = (codes, scales)
+
+        def project(n):
+            side = pieces[n][2]
+            codes, scales = map_mx[n]
+            rounded = proj_pool.tile([P, PIECE_ROWS, WIDTH, PACK], BF16, align_bytes=64)
+            proj[n] = rounded
+            for r in range(PIECE_ROWS):
+                cols = slice(r * WIDTH, (r + 1) * WIDTH)
+                bank = proj_psum.tile([P, O_TILES, WIDTH], F32, name="proj_bank")
+                for t in range(O_TILES):
+                    o_cols = slice(t * P, (t + 1) * P)
+                    for g in range(C_PASSES):
+                        nc.tensor.matmul_mx(
+                            out=bank[:, t, :],
+                            lhsT=w_codes[:, side, g, o_cols].bitcast(FP8X4),
+                            lhsT_scale=w_scales[:, side, g, o_cols],
+                            rhs=codes[:, g, cols].bitcast(FP8X4),
+                            rhs_scale=scales[:, g, cols],
+                            start=(g == 0),
+                            stop=(g == C_PASSES - 1),
+                        )
+                nc.scalar.copy(out=rounded[:, r, :, :], in_=bank[:].rearrange("p t w -> p w t"))
+
+        def quantise_projection(n):
+            codes = proj_mx_pool.tile([P, PIECE_COLS], U32, align_bytes=64, name="proj_codes")
+            scales = proj_mx_pool.tile([P, PIECE_COLS], U8, align_bytes=64, name="proj_scales")
+            nc.vector.quantize_mx(
+                out=codes[:].bitcast(FP8X4),
+                scales=scales[:],
+                in_=proj[n][:].rearrange("p r w j -> p (r w j)"),
+            )
+            proj_mx[n] = (codes, scales)
+
+        def scores(n_left, n_right):
+            b, part, side = pieces[n_left]
+            q_codes, q_scales = proj_mx[n_left]
+            k_codes, k_scales = proj_mx[n_right]
+            bank = dots_psum.tile([P, PIECE_ROWS, WIDTH], F32, name="dots_bank")
+            for r in range(PIECE_ROWS):
+                cols = slice(r * WIDTH, (r + 1) * WIDTH)
+                nc.tensor.matmul_mx(
+                    out=bank[:, r, :],
+                    lhsT=q_codes[:, cols].bitcast(FP8X4),
+                    lhsT_scale=q_scales[:, cols],
+                    rhs=k_codes[:, cols].bitcast(FP8X4),
+                    rhs_scale=k_scales[:, cols],
+                    start=True,
+                    stop=True,
+                )
+            dots = dots_pool.tile([P, PIECE_ROWS, WIDTH], F32)
+            nc.scalar.mul(out=dots[:], in_=bank[:], mul=SCALE)
+            image_rows = slice(part * PIECE_ROWS, (part + 1) * PIECE_ROWS)
+            nc.sync.dma_start(out=out[b, image_rows].rearrange("h w x -> w h x"), in_=dots[:])
+
+        with tc.manual_schedule():
+            for n in range(PREFETCH):
+                load_map(n)
+                if n < 2:
+                    load_weight(pieces[n][2])
+            for n in range(len(pieces) + 2):
+                if n + PREFETCH < len(pieces):
+                    load_map(n + PREFETCH)
+                if n < len(pieces):
+                    regroup(n)
+                if 1 <= n <= len(pieces):
+                    project(n - 1)
+                if n >= 2:
+                    quantise_projection(n - 2)
+                if n < len(pieces):
+                    quantise_map(n)
+                if n >= 2 and pieces[n - 2][2] == RIGHT:
+                    scores(n - 3, n - 2)

@@ -26,7 +26,7 @@ PIECE_COLS = PIECE_ROWS * WIDTH
 PIECES_PER_MAP = IMAGE_ROWS // PIECE_ROWS
 LEFT, RIGHT = 0, 1
 
-VECTOR_COLS = 384
+VECTOR_COLS = 400
 RUN = 4
 PREFETCH = 6
 

@@ -26,9 +26,10 @@ PIECE_COLS = PIECE_ROWS * WIDTH
 PIECES_PER_MAP = IMAGE_ROWS // PIECE_ROWS
 LEFT, RIGHT = 0, 1
 
-VECTOR_COLS = 400
+VECTOR_COLS = 384
 RUN = 4
 PREFETCH = 6
+SIDE_RUN = 2
 
 FLOPS = 2 * (2 * BATCH * IMAGE_ROWS * WIDTH * CHANNELS * INNER) + 2 * BATCH * IMAGE_ROWS * WIDTH * WIDTH * INNER
 
@@ -40,7 +41,11 @@ def tile_sttm_single_pa_t_kernel(
     maps = (left_feat, right_feat)
     weight_inputs = ((wq_words, wq_scales), (wk_words, wk_scales))
     pieces = [
-        (b, part, side) for b in range(BATCH) for part in range(PIECES_PER_MAP) for side in (LEFT, RIGHT)
+        (b, part, side)
+        for b in range(BATCH)
+        for first_part in range(0, PIECES_PER_MAP, SIDE_RUN)
+        for side in (LEFT, RIGHT)
+        for part in range(first_part, first_part + SIDE_RUN)
     ]
 
     with ExitStack() as ctx:
@@ -166,7 +171,7 @@ def tile_sttm_single_pa_t_kernel(
         with tc.manual_schedule():
             for n in range(PREFETCH):
                 load_map(n)
-                if n < 2:
+                if pieces[n][:2] == (0, 0):
                     load_weight(pieces[n][2])
             for n in range(len(pieces) + 2):
                 if n + PREFETCH < len(pieces):
@@ -180,4 +185,4 @@ def tile_sttm_single_pa_t_kernel(
                 if n < len(pieces):
                     quantise_map(n)
                 if n >= 2 and pieces[n - 2][2] == RIGHT:
-                    scores(n - 3, n - 2)
+                    scores(n - 2 - SIDE_RUN, n - 2)

@@ -27,7 +27,7 @@ PIECES_PER_MAP = IMAGE_ROWS // PIECE_ROWS
 LEFT, RIGHT = 0, 1
 
 VECTOR_COLS = 384
-RUN = 4
+RUN = 2
 PREFETCH = 6
 SIDE_RUN = 2
 

from contextlib import ExitStack

import concourse.mybir as mybir

BF16 = mybir.dt.bfloat16
F32 = mybir.dt.float32
I32 = mybir.dt.int32
U32 = mybir.dt.uint32
U8 = mybir.dt.uint8
FP8X4 = mybir.dt.float8_e4m3fn_x4

P = 128
PACK = 4
K_PASS = P * PACK

BATCH, CHANNELS, IMAGE_ROWS, WIDTH = 2, 1024, 16, 128
INNER = 512
SCALE = 0.125

C_PASSES = CHANNELS // K_PASS
O_TILES = INNER // P
assert O_TILES == PACK and INNER == K_PASS

PIECE_ROWS = 4
PIECE_COLS = PIECE_ROWS * WIDTH
PIECES_PER_MAP = IMAGE_ROWS // PIECE_ROWS
LEFT, RIGHT = 0, 1

VECTOR_COLS = 384
RUN = 2
PREFETCH = 6
SIDE_RUN = 2

FLOPS = 2 * (2 * BATCH * IMAGE_ROWS * WIDTH * CHANNELS * INNER) + 2 * BATCH * IMAGE_ROWS * WIDTH * WIDTH * INNER


def tile_sttm_single_pa_t_kernel(
    tc, left_feat, right_feat, wq_words, wq_scales, wk_words, wk_scales, out
):
    nc = tc.nc
    maps = (left_feat, right_feat)
    weight_inputs = ((wq_words, wq_scales), (wk_words, wk_scales))
    pieces = [
        (b, part, side)
        for b in range(BATCH)
        for first_part in range(0, PIECES_PER_MAP, SIDE_RUN)
        for side in (LEFT, RIGHT)
        for part in range(first_part, first_part + SIDE_RUN)
    ]

    with ExitStack() as ctx:
        weights = ctx.enter_context(tc.tile_pool(name="weights", bufs=1))
        raw_pool = ctx.enter_context(tc.tile_pool(name="raw", bufs=C_PASSES * (PREFETCH + 2)))
        grouped_pool = ctx.enter_context(tc.tile_pool(name="grouped", bufs=3))
        map_mx_pool = ctx.enter_context(tc.tile_pool(name="map_mx", bufs=3))
        proj_pool = ctx.enter_context(tc.tile_pool(name="proj", bufs=3))
        proj_mx_pool = ctx.enter_context(tc.tile_pool(name="proj_mx", bufs=4))
        dots_pool = ctx.enter_context(tc.tile_pool(name="dots", bufs=3))
        proj_psum = ctx.enter_context(tc.psum_pool(name="proj_psum", bufs=6))
        dots_psum = ctx.enter_context(tc.psum_pool(name="dots_psum", bufs=2))

        w_codes = weights.tile([P, 2, C_PASSES, INNER], U32, align_bytes=64)
        w_scales = weights.tile([P, 2, C_PASSES, INNER], U8, align_bytes=64)
        nc.vector.memset(w_scales[:].rearrange("p s g n -> p (s g n)").bitcast(I32), 0)

        raw = {}
        grouped = {}
        map_mx = {}
        proj = {}
        proj_mx = {}

        def load_weight(side):
            code_bytes, scale_bytes = weight_inputs[side]
            for quadrant in range(4):
                nc.sync.dma_start(
                    out=w_scales[32 * quadrant : 32 * quadrant + 4, side, :, :].bitcast(I32),
                    in_=scale_bytes[:, 4 * quadrant : 4 * quadrant + 4, :].rearrange("g r n -> r g n").bitcast(I32),
                )
            nc.sync.dma_start(
                out=w_codes[:, side, :, :].bitcast(I32),
                in_=code_bytes.rearrange("g p n t -> p g (n t)").bitcast(I32),
            )

        def load_map(n):
            b, part, side = pieces[n]
            by_pass = maps[side][b].rearrange("(g p j) h w -> g p j (h w)", p=P, j=PACK)
            for g in range(C_PASSES):
                rows = raw_pool.tile([P, PACK, PIECE_COLS], BF16)
                nc.sync.dma_start(
                    out=rows[:], in_=by_pass[g][:, :, part * PIECE_COLS : (part + 1) * PIECE_COLS]
                )
                raw[n, g] = rows

        def regroup(n):
            side_by_side = grouped_pool.tile([P, C_PASSES, PIECE_COLS, PACK], BF16, align_bytes=64)
            grouped[n] = side_by_side
            shares = (
                (nc.vector.tensor_copy, slice(0, VECTOR_COLS)),
                (nc.scalar.copy, slice(VECTOR_COLS, PIECE_COLS)),
            )
            for g in range(C_PASSES):
                for copy, cols in shares:
                    copy(
                        out=side_by_side[:, g, cols, :].rearrange("p (c i) j -> p c j i", i=RUN),
                        in_=raw[n, g][:, :, cols].rearrange("p j (c i) -> p c j i", i=RUN),
                    )

        def quantise_map(n):
            codes = map_mx_pool.tile([P, C_PASSES, PIECE_COLS], U32, align_bytes=64, name="map_codes")
            scales = map_mx_pool.tile([P, C_PASSES, PIECE_COLS], U8, align_bytes=64, name="map_scales")
            nc.vector.quantize_mx(
                out=codes[:].rearrange("p g c -> p (g c)").bitcast(FP8X4),
                scales=scales[:].rearrange("p g c -> p (g c)"),
                in_=grouped[n][:].rearrange("p g c j -> p (g c j)"),
            )
            map_mx[n] = (codes, scales)

        def project(n):
            side = pieces[n][2]
            codes, scales = map_mx[n]
            rounded = proj_pool.tile([P, PIECE_ROWS, WIDTH, PACK], BF16, align_bytes=64)
            proj[n] = rounded
            for r in range(PIECE_ROWS):
                cols = slice(r * WIDTH, (r + 1) * WIDTH)
                bank = proj_psum.tile([P, O_TILES, WIDTH], F32, name="proj_bank")
                for t in range(O_TILES):
                    o_cols = slice(t * P, (t + 1) * P)
                    for g in range(C_PASSES):
                        nc.tensor.matmul_mx(
                            out=bank[:, t, :],
                            lhsT=w_codes[:, side, g, o_cols].bitcast(FP8X4),
                            lhsT_scale=w_scales[:, side, g, o_cols],
                            rhs=codes[:, g, cols].bitcast(FP8X4),
                            rhs_scale=scales[:, g, cols],
                            start=(g == 0),
                            stop=(g == C_PASSES - 1),
                        )
                nc.scalar.copy(out=rounded[:, r, :, :], in_=bank[:].rearrange("p t w -> p w t"))

        def quantise_projection(n):
            codes = proj_mx_pool.tile([P, PIECE_COLS], U32, align_bytes=64, name="proj_codes")
            scales = proj_mx_pool.tile([P, PIECE_COLS], U8, align_bytes=64, name="proj_scales")
            nc.vector.quantize_mx(
                out=codes[:].bitcast(FP8X4),
                scales=scales[:],
                in_=proj[n][:].rearrange("p r w j -> p (r w j)"),
            )
            proj_mx[n] = (codes, scales)

        def scores(n_left, n_right):
            b, part, side = pieces[n_left]
            q_codes, q_scales = proj_mx[n_left]
            k_codes, k_scales = proj_mx[n_right]
            bank = dots_psum.tile([P, PIECE_ROWS, WIDTH], F32, name="dots_bank")
            for r in range(PIECE_ROWS):
                cols = slice(r * WIDTH, (r + 1) * WIDTH)
                nc.tensor.matmul_mx(
                    out=bank[:, r, :],
                    lhsT=q_codes[:, cols].bitcast(FP8X4),
                    lhsT_scale=q_scales[:, cols],
                    rhs=k_codes[:, cols].bitcast(FP8X4),
                    rhs_scale=k_scales[:, cols],
                    start=True,
                    stop=True,
                )
            dots = dots_pool.tile([P, PIECE_ROWS, WIDTH], F32)
            nc.scalar.mul(out=dots[:], in_=bank[:], mul=SCALE)
            image_rows = slice(part * PIECE_ROWS, (part + 1) * PIECE_ROWS)
            nc.sync.dma_start(out=out[b, image_rows].rearrange("h w x -> w h x"), in_=dots[:])

        with tc.manual_schedule():
            for n in range(PREFETCH):
                load_map(n)
                if pieces[n][:2] == (0, 0):
                    load_weight(pieces[n][2])
            for n in range(len(pieces) + 2):
                if n + PREFETCH < len(pieces):
                    load_map(n + PREFETCH)
                if n < len(pieces):
                    regroup(n)
                if 1 <= n <= len(pieces):
                    project(n - 1)
                if n >= 2:
                    quantise_projection(n - 2)
                if n < len(pieces):
                    quantise_map(n)
                if n >= 2 and pieces[n - 2][2] == RIGHT:
                    scores(n - 2 - SIDE_RUN, n - 2)
